import numpy as np
import ml_dtypes


def mxq(x, axis, fmt="e4m3"):
    dtype, down = {"e4m3": (ml_dtypes.float8_e4m3fn, 7), "e5m2": (ml_dtypes.float8_e5m2, 14)}[fmt]
    v = np.moveaxis(np.asarray(x, np.float32).astype(ml_dtypes.bfloat16).astype(np.float64), axis, -1)
    blocks = v.reshape(v.shape[:-1] + (-1, 32))
    amax = np.abs(blocks).max(-1, keepdims=True)
    byte = np.maximum(np.where(amax > 0, np.frexp(amax)[1] - 1 + 127, 0) - down, 1)
    scale = np.exp2(byte - 127.0)
    codes = (blocks / scale).astype(np.float32).astype(dtype).astype(np.float64)
    return np.moveaxis((codes * scale).reshape(v.shape), -1, axis)


WIDE = False


def mx_kscale(k):
    if not WIDE:
        return np.ones(k)
    levels = np.array([10, -10, 5, -5, 0])
    a = np.random.permutation(np.resize(levels, k // 512 * 4)).reshape(k // 512, 4)
    idx = np.arange(k)
    return np.exp2(a[idx // 512, idx % 128 // 32])


BF16 = ml_dtypes.bfloat16


def bf(x):
    return np.asarray(x, np.float32).astype(BF16)


def f64(x):
    return np.asarray(x).astype(np.float64)


B, CIN, H, W, COUT, N = 4, 512, 64, 64, 128, 9


def setup_inputs():
    s = mx_kscale(CIN)
    return {"x": bf(np.random.standard_normal((B, CIN, H, W)) * s[None, :, None, None]),
            "weights": bf(np.random.standard_normal((N, COUT, CIN, 1, 1)) * np.sqrt(N) / np.sqrt(CIN) / s[None, None, :, None, None]),
            "biases": bf(np.random.standard_normal((N, COUT)) * 0.5 * np.sqrt(N))}


def reference(x, weights, biases):
    w = np.mean(f64(weights), axis=0)[:, :, 0, 0]
    b = np.mean(f64(biases), axis=0)
    y = np.einsum('bchw,oc->bohw', mxq(f64(x), 1, "e4m3"), mxq(w, 1, "e4m3"), optimize=True) + b[None, :, None, None]
    return y

@@ -1,0 +1,175 @@
+from contextlib import ExitStack
+
+import concourse.mybir as mybir
+from concourse.masks import make_identity
+
+BF16 = mybir.dt.bfloat16
+F32 = mybir.dt.float32
+U32 = mybir.dt.uint32
+U8 = mybir.dt.uint8
+FP8X4 = mybir.dt.float8_e4m3fn_x4
+
+IMAGES = 4
+CIN = 512
+PIXELS = 64 * 64
+COUT = 128
+LAYERS = 9
+
+P = 128
+PACK = 4
+assert CIN == P * PACK and COUT == P
+
+LOAD_COLS = 2048
+SLAB_COLS = 1024
+BANK_COLS = 512
+RUN = 4
+
+PIECES = IMAGES * PIXELS // LOAD_COLS
+PIECES_PER_IMAGE = PIXELS // LOAD_COLS
+SLABS = IMAGES * PIXELS // SLAB_COLS
+SLABS_PER_PIECE = LOAD_COLS // SLAB_COLS
+BANKS_PER_SLAB = SLAB_COLS // BANK_COLS
+
+VECTOR_COLS = 688
+
+X_BUFS = 6
+
+FLOPS = 2 * IMAGES * PIXELS * CIN * COUT
+
+
+def tile_conv_1x1_9_layer_kernel(tc, x, weights, biases, out):
+    nc = tc.nc
+    identity_fn = mybir.ActivationFunctionType.Identity
+
+    x_view = x.rearrange("n (p t) h v -> n p t (h v)", t=PACK)
+    w_view = weights.rearrange("i o c a b -> o i (c a b)")
+    y_view = out.rearrange("n o h v -> n o (h v)")
+
+    with ExitStack() as ctx:
+        const = ctx.enter_context(tc.tile_pool(name="const", bufs=1))
+        x_pool = ctx.enter_context(tc.tile_pool(name="x", bufs=X_BUFS))
+        y_pool = ctx.enter_context(tc.tile_pool(name="y", bufs=PIECES))
+        slab_pool = ctx.enter_context(tc.tile_pool(name="slab", bufs=3))
+        prep_psum = ctx.enter_context(tc.psum_pool(name="prep_psum", bufs=1))
+        acc_psum = ctx.enter_context(tc.psum_pool(name="acc_psum", bufs=6))
+
+        w_raw = const.tile([P, LAYERS, CIN], BF16)
+        nc.scalar.dma_start(out=w_raw[:], in_=w_view)
+        bias_rows = const.tile([P, COUT], BF16)
+        nc.vector.memset(bias_rows[:], 0.0)
+        nc.scalar.dma_start(out=bias_rows[0:LAYERS, :], in_=biases)
+
+        x_pieces = []
+        for piece in range(PIECES):
+            image, part = divmod(piece, PIECES_PER_IMAGE)
+            x_piece = x_pool.tile([P, PACK, LOAD_COLS], BF16, name="x_piece")
+            nc.sync.dma_start(
+                out=x_piece[:],
+                in_=x_view[image, :, :, part * LOAD_COLS : (part + 1) * LOAD_COLS],
+            )
+            x_pieces.append(x_piece)
+
+        ident = const.tile([P, P], BF16)
+        make_identity(nc, ident[:])
+        w_by_code = w_raw[:].rearrange("o i (p t) -> o i t p", t=PACK)
+        w_sum = prep_psum.tile([P, PACK, COUT], F32)
+        for t in range(PACK):
+            for i in range(LAYERS):
+                nc.tensor.matmul(
+                    out=w_sum[:, t, :],
+                    lhsT=w_by_code[:, i, t, :],
+                    rhs=ident[:],
+                    start=(i == 0),
+                    stop=(i == LAYERS - 1),
+                )
+        w_grouped = const.tile([P, COUT, PACK], BF16, align_bytes=64)
+        nc.vector.tensor_scalar_mul(
+            out=w_grouped[:], in0=w_sum[:].rearrange("p t o -> p o t"), scalar1=1.0 / LAYERS
+        )
+        w_codes = const.tile([P, COUT], U32, align_bytes=64)
+        w_scales = const.tile([P, COUT], U8, align_bytes=64)
+        nc.vector.quantize_mx(
+            out=w_codes[:].bitcast(FP8X4),
+            scales=w_scales[:],
+            in_=w_grouped[:].rearrange("p o t -> p (o t)"),
+        )
+
+        ones = const.tile([P, P], BF16)
+        nc.vector.memset(ones[:], 1.0)
+        bias_sum = prep_psum.tile([P, P], F32)
+        nc.tensor.matmul(out=bias_sum[:], lhsT=bias_rows[:], rhs=ones[:], start=True, stop=True)
+        bias = const.tile([P, 1], F32)
+        nc.vector.tensor_scalar_mul(out=bias[:], in0=bias_sum[:, 0:1], scalar1=1.0 / LAYERS)
+
+        grouped = {}
+        codes = {}
+        scales = {}
+        y_pieces = {}
+
+        def regroup(s):
+            piece, part = divmod(s, SLABS_PER_PIECE)
+            first = part * SLAB_COLS
+            src = x_pieces[piece]
+            dst = slab_pool.tile([P, SLAB_COLS, PACK], BF16, name="grouped", align_bytes=64)
+            nc.vector.tensor_copy(
+                out=dst[:, 0:VECTOR_COLS, :].rearrange("p (c i) t -> p c t i", i=RUN),
+                in_=src[:, :, first : first + VECTOR_COLS].rearrange(
+                    "p t (c i) -> p c t i", i=RUN
+                ),
+            )
+            nc.scalar.copy(
+                out=dst[:, VECTOR_COLS:SLAB_COLS, :].rearrange("p (c i) t -> p c t i", i=RUN),
+                in_=src[:, :, first + VECTOR_COLS : first + SLAB_COLS].rearrange(
+                    "p t (c i) -> p c t i", i=RUN
+                ),
+            )
+            grouped[s] = dst
+
+        def quantise(s):
+            codes[s] = slab_pool.tile([P, SLAB_COLS], U32, name="codes", align_bytes=64)
+            scales[s] = slab_pool.tile([P, SLAB_COLS], U8, name="scales", align_bytes=64)
+            nc.vector.quantize_mx(
+                out=codes[s][:].bitcast(FP8X4),
+                scales=scales[s][:],
+                in_=grouped[s][:].rearrange("p c t -> p (c t)"),
+            )
+
+        def multiply_and_store(s):
+            piece, part = divmod(s, SLABS_PER_PIECE)
+            if part == 0:
+                y_pieces[piece] = y_pool.tile([P, LOAD_COLS], F32, name="y_piece")
+            y_piece = y_pieces[piece]
+            for bank in range(BANKS_PER_SLAB):
+                cols = slice(bank * BANK_COLS, (bank + 1) * BANK_COLS)
+                acc = acc_psum.tile([P, BANK_COLS], F32, name="acc")
+                nc.tensor.matmul_mx(
+                    out=acc[:],
+                    lhsT=w_codes[:].bitcast(FP8X4),
+                    lhsT_scale=w_scales[:],
+                    rhs=codes[s][:, cols].bitcast(FP8X4),
+                    rhs_scale=scales[s][:, cols],
+                    start=True,
+                    stop=True,
+                )
+                first = part * SLAB_COLS + bank * BANK_COLS
+                nc.scalar.activation(
+                    out=y_piece[:, first : first + BANK_COLS],
+                    in_=acc[:],
+                    func=identity_fn,
+                    bias=bias[:, 0:1],
+                    scale=1.0,
+                )
+            if part == SLABS_PER_PIECE - 1:
+                image, image_part = divmod(piece, PIECES_PER_IMAGE)
+                nc.sync.dma_start(
+                    out=y_view[image, :, image_part * LOAD_COLS : (image_part + 1) * LOAD_COLS],
+                    in_=y_piece[:],
+                )
+
+        for step in range(SLABS + 2):
+            if step < SLABS:
+                regroup(step)
+            if 1 <= step <= SLABS:
+                quantise(step - 1)
+            if step >= 2:
+                multiply_and_store(step - 2)

@@ -53,8 +53,10 @@ def tile_conv_1x1_9_layer_kernel(tc, x, weights, biases, out):
         prep_psum = ctx.enter_context(tc.psum_pool(name="prep_psum", bufs=1))
         acc_psum = ctx.enter_context(tc.psum_pool(name="acc_psum", bufs=6))
 
+        ctx.enter_context(tc.manual_schedule())
+
         w_raw = const.tile([P, LAYERS, CIN], BF16)
-        nc.scalar.dma_start(out=w_raw[:], in_=w_view)
+        nc.sync.dma_start(out=w_raw[:], in_=w_view)
         bias_rows = const.tile([P, COUT], BF16)
         nc.vector.memset(bias_rows[:], 0.0)
         nc.scalar.dma_start(out=bias_rows[0:LAYERS, :], in_=biases)
@@ -82,24 +84,26 @@ def tile_conv_1x1_9_layer_kernel(tc, x, weights, biases, out):
                     start=(i == 0),
                     stop=(i == LAYERS - 1),
                 )
-        w_grouped = const.tile([P, COUT, PACK], BF16, align_bytes=64)
-        nc.vector.tensor_scalar_mul(
-            out=w_grouped[:], in0=w_sum[:].rearrange("p t o -> p o t"), scalar1=1.0 / LAYERS
-        )
-        w_codes = const.tile([P, COUT], U32, align_bytes=64)
-        w_scales = const.tile([P, COUT], U8, align_bytes=64)
-        nc.vector.quantize_mx(
-            out=w_codes[:].bitcast(FP8X4),
-            scales=w_scales[:],
-            in_=w_grouped[:].rearrange("p o t -> p (o t)"),
-        )
-
         ones = const.tile([P, P], BF16)
         nc.vector.memset(ones[:], 1.0)
         bias_sum = prep_psum.tile([P, P], F32)
         nc.tensor.matmul(out=bias_sum[:], lhsT=bias_rows[:], rhs=ones[:], start=True, stop=True)
+
+        w_grouped = const.tile([P, COUT, PACK], BF16, align_bytes=64)
+        w_codes = const.tile([P, COUT], U32, align_bytes=64)
+        w_scales = const.tile([P, COUT], U8, align_bytes=64)
         bias = const.tile([P, 1], F32)
-        nc.vector.tensor_scalar_mul(out=bias[:], in0=bias_sum[:, 0:1], scalar1=1.0 / LAYERS)
+
+        def finish_weights():
+            nc.vector.tensor_scalar_mul(
+                out=w_grouped[:], in0=w_sum[:].rearrange("p t o -> p o t"), scalar1=1.0 / LAYERS
+            )
+            nc.vector.tensor_scalar_mul(out=bias[:], in0=bias_sum[:, 0:1], scalar1=1.0 / LAYERS)
+            nc.vector.quantize_mx(
+                out=w_codes[:].bitcast(FP8X4),
+                scales=w_scales[:],
+                in_=w_grouped[:].rearrange("p o t -> p (o t)"),
+            )
 
         grouped = {}
         codes = {}
@@ -169,6 +173,8 @@ def tile_conv_1x1_9_layer_kernel(tc, x, weights, biases, out):
         for step in range(SLABS + 2):
             if step < SLABS:
                 regroup(step)
+            if step == 0:
+                finish_weights()
             if 1 <= step <= SLABS:
                 quantise(step - 1)
             if step >= 2:

@@ -24,6 +24,7 @@ SLAB_COLS = 1024
 BANK_COLS = 512
 RUN = 4
 
+SPLIT_PIECES = 2
 PIECES = IMAGES * PIXELS // LOAD_COLS
 PIECES_PER_IMAGE = PIXELS // LOAD_COLS
 SLABS = IMAGES * PIXELS // SLAB_COLS
@@ -61,15 +62,24 @@ def tile_conv_1x1_9_layer_kernel(tc, x, weights, biases, out):
         nc.vector.memset(bias_rows[:], 0.0)
         nc.scalar.dma_start(out=bias_rows[0:LAYERS, :], in_=biases)
 
-        x_pieces = []
+        x_slabs = []
         for piece in range(PIECES):
             image, part = divmod(piece, PIECES_PER_IMAGE)
-            x_piece = x_pool.tile([P, PACK, LOAD_COLS], BF16, name="x_piece")
-            nc.sync.dma_start(
-                out=x_piece[:],
-                in_=x_view[image, :, :, part * LOAD_COLS : (part + 1) * LOAD_COLS],
-            )
-            x_pieces.append(x_piece)
+            x_piece = x_pool.tile([P, PACK * LOAD_COLS], BF16, name="x_piece")
+            first = part * LOAD_COLS
+            if piece < SPLIT_PIECES:
+                halves = x_piece[:].rearrange("p (h t c) -> p h t c", h=SLABS_PER_PIECE, t=PACK)
+                for h in range(SLABS_PER_PIECE):
+                    nc.sync.dma_start(
+                        out=halves[:, h, :, :],
+                        in_=x_view[image, :, :, first + h * SLAB_COLS : first + (h + 1) * SLAB_COLS],
+                    )
+                    x_slabs.append(halves[:, h, :, :])
+            else:
+                whole = x_piece[:].rearrange("p (t c) -> p t c", t=PACK)
+                nc.sync.dma_start(out=whole, in_=x_view[image, :, :, first : first + LOAD_COLS])
+                for h in range(SLABS_PER_PIECE):
+                    x_slabs.append(whole[:, :, h * SLAB_COLS : (h + 1) * SLAB_COLS])
 
         ident = const.tile([P, P], BF16)
         make_identity(nc, ident[:])
@@ -111,19 +121,17 @@ def tile_conv_1x1_9_layer_kernel(tc, x, weights, biases, out):
         y_pieces = {}
 
         def regroup(s):
-            piece, part = divmod(s, SLABS_PER_PIECE)
-            first = part * SLAB_COLS
-            src = x_pieces[piece]
+            src = x_slabs[s]
             dst = slab_pool.tile([P, SLAB_COLS, PACK], BF16, name="grouped", align_bytes=64)
             nc.vector.tensor_copy(
                 out=dst[:, 0:VECTOR_COLS, :].rearrange("p (c i) t -> p c t i", i=RUN),
-                in_=src[:, :, first : first + VECTOR_COLS].rearrange(
+                in_=src[:, :, 0:VECTOR_COLS].rearrange(
                     "p t (c i) -> p c t i", i=RUN
                 ),
             )
             nc.scalar.copy(
                 out=dst[:, VECTOR_COLS:SLAB_COLS, :].rearrange("p (c i) t -> p c t i", i=RUN),
-                in_=src[:, :, first + VECTOR_COLS : first + SLAB_COLS].rearrange(
+                in_=src[:, :, VECTOR_COLS:SLAB_COLS].rearrange(
                     "p t (c i) -> p c t i", i=RUN
                 ),
             )
@@ -156,15 +164,26 @@ def tile_conv_1x1_9_layer_kernel(tc, x, weights, biases, out):
                     stop=True,
                 )
                 first = part * SLAB_COLS + bank * BANK_COLS
-                nc.scalar.activation(
-                    out=y_piece[:, first : first + BANK_COLS],
-                    in_=acc[:],
-                    func=identity_fn,
-                    bias=bias[:, 0:1],
-                    scale=1.0,
+                if s == SLABS - 1 and bank == BANKS_PER_SLAB - 1:
+                    nc.vector.tensor_scalar_add(
+                        out=y_piece[:, first : first + BANK_COLS], in0=acc[:], scalar1=bias[:, 0:1]
+                    )
+                else:
+                    nc.scalar.activation(
+                        out=y_piece[:, first : first + BANK_COLS],
+                        in_=acc[:],
+                        func=identity_fn,
+                        bias=bias[:, 0:1],
+                        scale=1.0,
+                    )
+            image, image_part = divmod(piece, PIECES_PER_IMAGE)
+            if piece == PIECES - 1:
+                lo = part * SLAB_COLS
+                nc.sync.dma_start(
+                    out=y_view[image, :, image_part * LOAD_COLS + lo : image_part * LOAD_COLS + lo + SLAB_COLS],
+                    in_=y_piece[:, lo : lo + SLAB_COLS],
                 )
-            if part == SLABS_PER_PIECE - 1:
-                image, image_part = divmod(piece, PIECES_PER_IMAGE)
+            elif part == SLABS_PER_PIECE - 1:
                 nc.sync.dma_start(
                     out=y_view[image, :, image_part * LOAD_COLS : (image_part + 1) * LOAD_COLS],
                     in_=y_piece[:],

@@ -33,7 +33,7 @@ BANKS_PER_SLAB = SLAB_COLS // BANK_COLS
 
 VECTOR_COLS = 688
 
-X_BUFS = 6
+BIG_BUFS = 10
 
 FLOPS = 2 * IMAGES * PIXELS * CIN * COUT
 
@@ -48,8 +48,7 @@ def tile_conv_1x1_9_layer_kernel(tc, x, weights, biases, out):
 
     with ExitStack() as ctx:
         const = ctx.enter_context(tc.tile_pool(name="const", bufs=1))
-        x_pool = ctx.enter_context(tc.tile_pool(name="x", bufs=X_BUFS))
-        y_pool = ctx.enter_context(tc.tile_pool(name="y", bufs=PIECES))
+        big_pool = ctx.enter_context(tc.tile_pool(name="big", bufs=BIG_BUFS))
         slab_pool = ctx.enter_context(tc.tile_pool(name="slab", bufs=3))
         prep_psum = ctx.enter_context(tc.psum_pool(name="prep_psum", bufs=1))
         acc_psum = ctx.enter_context(tc.psum_pool(name="acc_psum", bufs=6))
@@ -60,24 +59,25 @@ def tile_conv_1x1_9_layer_kernel(tc, x, weights, biases, out):
         nc.sync.dma_start(out=w_raw[:], in_=w_view)
         bias_rows = const.tile([P, COUT], BF16)
         nc.vector.memset(bias_rows[:], 0.0)
-        nc.scalar.dma_start(out=bias_rows[0:LAYERS, :], in_=biases)
+        nc.gpsimd.dma_start(out=bias_rows[0:LAYERS, :], in_=biases)
 
         x_slabs = []
         for piece in range(PIECES):
             image, part = divmod(piece, PIECES_PER_IMAGE)
-            x_piece = x_pool.tile([P, PACK * LOAD_COLS], BF16, name="x_piece")
+            x_piece = big_pool.tile([P, PACK * LOAD_COLS], BF16, name="big")
             first = part * LOAD_COLS
+            queue = nc.scalar if piece % 2 == 0 else nc.sync
             if piece < SPLIT_PIECES:
                 halves = x_piece[:].rearrange("p (h t c) -> p h t c", h=SLABS_PER_PIECE, t=PACK)
                 for h in range(SLABS_PER_PIECE):
-                    nc.sync.dma_start(
+                    queue.dma_start(
                         out=halves[:, h, :, :],
                         in_=x_view[image, :, :, first + h * SLAB_COLS : first + (h + 1) * SLAB_COLS],
                     )
                     x_slabs.append(halves[:, h, :, :])
             else:
                 whole = x_piece[:].rearrange("p (t c) -> p t c", t=PACK)
-                nc.sync.dma_start(out=whole, in_=x_view[image, :, :, first : first + LOAD_COLS])
+                queue.dma_start(out=whole, in_=x_view[image, :, :, first : first + LOAD_COLS])
                 for h in range(SLABS_PER_PIECE):
                     x_slabs.append(whole[:, :, h * SLAB_COLS : (h + 1) * SLAB_COLS])
 
@@ -118,7 +118,7 @@ def tile_conv_1x1_9_layer_kernel(tc, x, weights, biases, out):
         grouped = {}
         codes = {}
         scales = {}
-        y_pieces = {}
+        y_images = {}
 
         def regroup(s):
             src = x_slabs[s]
@@ -148,9 +148,10 @@ def tile_conv_1x1_9_layer_kernel(tc, x, weights, biases, out):
 
         def multiply_and_store(s):
             piece, part = divmod(s, SLABS_PER_PIECE)
-            if part == 0:
-                y_pieces[piece] = y_pool.tile([P, LOAD_COLS], F32, name="y_piece")
-            y_piece = y_pieces[piece]
+            image, image_part = divmod(piece, PIECES_PER_IMAGE)
+            if part == 0 and image_part == 0:
+                y_images[image] = big_pool.tile([P, PIXELS], F32, name="big")
+            y_piece = y_images[image][:, image_part * LOAD_COLS : (image_part + 1) * LOAD_COLS]
             for bank in range(BANKS_PER_SLAB):
                 cols = slice(bank * BANK_COLS, (bank + 1) * BANK_COLS)
                 acc = acc_psum.tile([P, BANK_COLS], F32, name="acc")
@@ -176,17 +177,18 @@ def tile_conv_1x1_9_layer_kernel(tc, x, weights, biases, out):
                         bias=bias[:, 0:1],
                         scale=1.0,
                     )
-            image, image_part = divmod(piece, PIECES_PER_IMAGE)
             if piece == PIECES - 1:
                 lo = part * SLAB_COLS
-                nc.sync.dma_start(
+                queue = nc.scalar if part == 0 else nc.sync
+                queue.dma_start(
                     out=y_view[image, :, image_part * LOAD_COLS + lo : image_part * LOAD_COLS + lo + SLAB_COLS],
                     in_=y_piece[:, lo : lo + SLAB_COLS],
                 )
             elif part == SLABS_PER_PIECE - 1:
-                nc.sync.dma_start(
+                queue = nc.scalar if piece % 2 == 0 else nc.sync
+                queue.dma_start(
                     out=y_view[image, :, image_part * LOAD_COLS : (image_part + 1) * LOAD_COLS],
-                    in_=y_piece[:],
+                    in_=y_piece,
                 )
 
         for step in range(SLABS + 2):

@@ -24,7 +24,8 @@ SLAB_COLS = 1024
 BANK_COLS = 512
 RUN = 4
 
-SPLIT_PIECES = 2
+SPLIT_PIECES = 1
+WHOLE_IMAGES = 1
 PIECES = IMAGES * PIXELS // LOAD_COLS
 PIECES_PER_IMAGE = PIXELS // LOAD_COLS
 SLABS = IMAGES * PIXELS // SLAB_COLS
@@ -33,7 +34,7 @@ BANKS_PER_SLAB = SLAB_COLS // BANK_COLS
 
 VECTOR_COLS = 688
 
-BIG_BUFS = 10
+BIG_BUFS = 8
 
 FLOPS = 2 * IMAGES * PIXELS * CIN * COUT
 
@@ -49,6 +50,7 @@ def tile_conv_1x1_9_layer_kernel(tc, x, weights, biases, out):
     with ExitStack() as ctx:
         const = ctx.enter_context(tc.tile_pool(name="const", bufs=1))
         big_pool = ctx.enter_context(tc.tile_pool(name="big", bufs=BIG_BUFS))
+        image_pool = ctx.enter_context(tc.tile_pool(name="image", bufs=WHOLE_IMAGES))
         slab_pool = ctx.enter_context(tc.tile_pool(name="slab", bufs=3))
         prep_psum = ctx.enter_context(tc.psum_pool(name="prep_psum", bufs=1))
         acc_psum = ctx.enter_context(tc.psum_pool(name="acc_psum", bufs=6))
@@ -59,27 +61,32 @@ def tile_conv_1x1_9_layer_kernel(tc, x, weights, biases, out):
         nc.sync.dma_start(out=w_raw[:], in_=w_view)
         bias_rows = const.tile([P, COUT], BF16)
         nc.vector.memset(bias_rows[:], 0.0)
-        nc.gpsimd.dma_start(out=bias_rows[0:LAYERS, :], in_=biases)
+        nc.scalar.dma_start(out=bias_rows[0:LAYERS, :], in_=biases)
 
         x_slabs = []
-        for piece in range(PIECES):
+        for piece in range(PIECES - WHOLE_IMAGES * PIECES_PER_IMAGE):
             image, part = divmod(piece, PIECES_PER_IMAGE)
             x_piece = big_pool.tile([P, PACK * LOAD_COLS], BF16, name="big")
             first = part * LOAD_COLS
-            queue = nc.scalar if piece % 2 == 0 else nc.sync
             if piece < SPLIT_PIECES:
                 halves = x_piece[:].rearrange("p (h t c) -> p h t c", h=SLABS_PER_PIECE, t=PACK)
                 for h in range(SLABS_PER_PIECE):
-                    queue.dma_start(
+                    nc.sync.dma_start(
                         out=halves[:, h, :, :],
                         in_=x_view[image, :, :, first + h * SLAB_COLS : first + (h + 1) * SLAB_COLS],
                     )
                     x_slabs.append(halves[:, h, :, :])
             else:
                 whole = x_piece[:].rearrange("p (t c) -> p t c", t=PACK)
-                queue.dma_start(out=whole, in_=x_view[image, :, :, first : first + LOAD_COLS])
+                nc.sync.dma_start(out=whole, in_=x_view[image, :, :, first : first + LOAD_COLS])
                 for h in range(SLABS_PER_PIECE):
                     x_slabs.append(whole[:, :, h * SLAB_COLS : (h + 1) * SLAB_COLS])
+        for image in range(IMAGES - WHOLE_IMAGES, IMAGES):
+            x_image = image_pool.tile([P, PACK * PIXELS], BF16, name="x_image")
+            whole = x_image[:].rearrange("p (t c) -> p t c", t=PACK)
+            nc.sync.dma_start(out=whole, in_=x_view[image, :, :, :])
+            for h in range(PIXELS // SLAB_COLS):
+                x_slabs.append(whole[:, :, h * SLAB_COLS : (h + 1) * SLAB_COLS])
 
         ident = const.tile([P, P], BF16)
         make_identity(nc, ident[:])
@@ -179,17 +186,18 @@ def tile_conv_1x1_9_layer_kernel(tc, x, weights, biases, out):
                     )
             if piece == PIECES - 1:
                 lo = part * SLAB_COLS
-                queue = nc.scalar if part == 0 else nc.sync
-                queue.dma_start(
+                nc.sync.dma_start(
                     out=y_view[image, :, image_part * LOAD_COLS + lo : image_part * LOAD_COLS + lo + SLAB_COLS],
                     in_=y_piece[:, lo : lo + SLAB_COLS],
                 )
-            elif part == SLABS_PER_PIECE - 1:
-                queue = nc.scalar if piece % 2 == 0 else nc.sync
-                queue.dma_start(
-                    out=y_view[image, :, image_part * LOAD_COLS : (image_part + 1) * LOAD_COLS],
-                    in_=y_piece,
-                )
+            elif image == IMAGES - 1:
+                if part == SLABS_PER_PIECE - 1:
+                    nc.sync.dma_start(
+                        out=y_view[image, :, image_part * LOAD_COLS : (image_part + 1) * LOAD_COLS],
+                        in_=y_piece,
+                    )
+            elif part == SLABS_PER_PIECE - 1 and image_part == PIECES_PER_IMAGE - 1:
+                nc.sync.dma_start(out=y_view[image, :, :], in_=y_images[image][:])
 
         for step in range(SLABS + 2):
             if step < SLABS:

@@ -1,10 +1,10 @@
 from contextlib import ExitStack
 
 import concourse.mybir as mybir
-from concourse.masks import make_identity
 
 BF16 = mybir.dt.bfloat16
 F32 = mybir.dt.float32
+I32 = mybir.dt.int32
 U32 = mybir.dt.uint32
 U8 = mybir.dt.uint8
 FP8X4 = mybir.dt.float8_e4m3fn_x4
@@ -24,7 +24,7 @@ SLAB_COLS = 1024
 BANK_COLS = 512
 RUN = 4
 
-SPLIT_PIECES = 1
+WEIGHTS_STEP = 2
 WHOLE_IMAGES = 1
 PIECES = IMAGES * PIXELS // LOAD_COLS
 PIECES_PER_IMAGE = PIXELS // LOAD_COLS
@@ -44,7 +44,7 @@ def tile_conv_1x1_9_layer_kernel(tc, x, weights, biases, out):
     identity_fn = mybir.ActivationFunctionType.Identity
 
     x_view = x.rearrange("n (p t) h v -> n p t (h v)", t=PACK)
-    w_view = weights.rearrange("i o c a b -> o i (c a b)")
+    w_view = weights.rearrange("i o c a b -> (i o) (c a b)").rearrange("(q j) c -> q j c", j=LAYERS)
     y_view = out.rearrange("n o h v -> n o (h v)")
 
     with ExitStack() as ctx:
@@ -58,7 +58,6 @@ def tile_conv_1x1_9_layer_kernel(tc, x, weights, biases, out):
         ctx.enter_context(tc.manual_schedule())
 
         w_raw = const.tile([P, LAYERS, CIN], BF16)
-        nc.sync.dma_start(out=w_raw[:], in_=w_view)
         bias_rows = const.tile([P, COUT], BF16)
         nc.vector.memset(bias_rows[:], 0.0)
         nc.scalar.dma_start(out=bias_rows[0:LAYERS, :], in_=biases)
@@ -68,19 +67,12 @@ def tile_conv_1x1_9_layer_kernel(tc, x, weights, biases, out):
             image, part = divmod(piece, PIECES_PER_IMAGE)
             x_piece = big_pool.tile([P, PACK * LOAD_COLS], BF16, name="big")
             first = part * LOAD_COLS
-            if piece < SPLIT_PIECES:
-                halves = x_piece[:].rearrange("p (h t c) -> p h t c", h=SLABS_PER_PIECE, t=PACK)
-                for h in range(SLABS_PER_PIECE):
-                    nc.sync.dma_start(
-                        out=halves[:, h, :, :],
-                        in_=x_view[image, :, :, first + h * SLAB_COLS : first + (h + 1) * SLAB_COLS],
-                    )
-                    x_slabs.append(halves[:, h, :, :])
-            else:
-                whole = x_piece[:].rearrange("p (t c) -> p t c", t=PACK)
-                nc.sync.dma_start(out=whole, in_=x_view[image, :, :, first : first + LOAD_COLS])
-                for h in range(SLABS_PER_PIECE):
-                    x_slabs.append(whole[:, :, h * SLAB_COLS : (h + 1) * SLAB_COLS])
+            whole = x_piece[:].rearrange("p (t c) -> p t c", t=PACK)
+            nc.sync.dma_start(out=whole, in_=x_view[image, :, :, first : first + LOAD_COLS])
+            for h in range(SLABS_PER_PIECE):
+                x_slabs.append(whole[:, :, h * SLAB_COLS : (h + 1) * SLAB_COLS])
+            if piece == 0:
+                nc.sync.dma_start(out=w_raw[:], in_=w_view)
         for image in range(IMAGES - WHOLE_IMAGES, IMAGES):
             x_image = image_pool.tile([P, PACK * PIXELS], BF16, name="x_image")
             whole = x_image[:].rearrange("p (t c) -> p t c", t=PACK)
@@ -88,18 +80,32 @@ def tile_conv_1x1_9_layer_kernel(tc, x, weights, biases, out):
             for h in range(PIXELS // SLAB_COLS):
                 x_slabs.append(whole[:, :, h * SLAB_COLS : (h + 1) * SLAB_COLS])
 
-        ident = const.tile([P, P], BF16)
-        make_identity(nc, ident[:])
-        w_by_code = w_raw[:].rearrange("o i (p t) -> o i t p", t=PACK)
+        pick_index = const.tile([P, LAYERS, COUT], I32)
+        nc.gpsimd.iota(
+            pick_index[:], pattern=[[1, LAYERS], [-1, COUT]], base=COUT, channel_multiplier=LAYERS
+        )
+        pick_low = const.tile([P, LAYERS, COUT], I32)
+        nc.vector.tensor_scalar(
+            out=pick_low[:],
+            in0=pick_index[:],
+            scalar1=COUT - 1,
+            scalar2=None,
+            op0=mybir.AluOpType.bitwise_and,
+        )
+        pick = const.tile([P, LAYERS, COUT], BF16)
+        nc.vector.tensor_scalar(
+            out=pick[:], in0=pick_low[:], scalar1=0.0, scalar2=None, op0=mybir.AluOpType.is_equal
+        )
+        w_by_code = w_raw[:].rearrange("q j (p t) -> q j t p", t=PACK)
         w_sum = prep_psum.tile([P, PACK, COUT], F32)
         for t in range(PACK):
-            for i in range(LAYERS):
+            for j in range(LAYERS):
                 nc.tensor.matmul(
                     out=w_sum[:, t, :],
-                    lhsT=w_by_code[:, i, t, :],
-                    rhs=ident[:],
-                    start=(i == 0),
-                    stop=(i == LAYERS - 1),
+                    lhsT=w_by_code[:, j, t, :],
+                    rhs=pick[:, j, :],
+                    start=(j == 0),
+                    stop=(j == LAYERS - 1),
                 )
         ones = const.tile([P, P], BF16)
         nc.vector.memset(ones[:], 1.0)
@@ -202,9 +208,11 @@ def tile_conv_1x1_9_layer_kernel(tc, x, weights, biases, out):
         for step in range(SLABS + 2):
             if step < SLABS:
                 regroup(step)
-            if step == 0:
-                finish_weights()
             if 1 <= step <= SLABS:
                 quantise(step - 1)
-            if step >= 2:
+            if step == WEIGHTS_STEP:
+                finish_weights()
+            if step == WEIGHTS_STEP + 1:
+                multiply_and_store(step - 3)
+            if step > WEIGHTS_STEP:
                 multiply_and_store(step - 2)

@@ -25,7 +25,7 @@ BANK_COLS = 512
 RUN = 4
 
 WEIGHTS_STEP = 2
-WHOLE_IMAGES = 1
+WHOLE_IMAGES = 2
 PIECES = IMAGES * PIXELS // LOAD_COLS
 PIECES_PER_IMAGE = PIXELS // LOAD_COLS
 SLABS = IMAGES * PIXELS // SLAB_COLS
@@ -34,7 +34,7 @@ BANKS_PER_SLAB = SLAB_COLS // BANK_COLS
 
 VECTOR_COLS = 688
 
-BIG_BUFS = 8
+BIG_BUFS = 6
 
 FLOPS = 2 * IMAGES * PIXELS * CIN * COUT
 

@@ -28,9 +28,8 @@ WEIGHTS_STEP = 2
 WHOLE_IMAGES = 2
 PIECES = IMAGES * PIXELS // LOAD_COLS
 PIECES_PER_IMAGE = PIXELS // LOAD_COLS
-SLABS = IMAGES * PIXELS // SLAB_COLS
-SLABS_PER_PIECE = LOAD_COLS // SLAB_COLS
-BANKS_PER_SLAB = SLAB_COLS // BANK_COLS
+LAST_IMAGE_STORES = (2048, 1024, 512, 512)
+assert sum(LAST_IMAGE_STORES) == PIXELS
 
 VECTOR_COLS = 688
 
@@ -62,23 +61,24 @@ def tile_conv_1x1_9_layer_kernel(tc, x, weights, biases, out):
         nc.vector.memset(bias_rows[:], 0.0)
         nc.scalar.dma_start(out=bias_rows[0:LAYERS, :], in_=biases)
 
-        x_slabs = []
+        x_images = {image: [] for image in range(IMAGES)}
+        x_cols = {}
         for piece in range(PIECES - WHOLE_IMAGES * PIECES_PER_IMAGE):
             image, part = divmod(piece, PIECES_PER_IMAGE)
             x_piece = big_pool.tile([P, PACK * LOAD_COLS], BF16, name="big")
             first = part * LOAD_COLS
             whole = x_piece[:].rearrange("p (t c) -> p t c", t=PACK)
             nc.sync.dma_start(out=whole, in_=x_view[image, :, :, first : first + LOAD_COLS])
-            for h in range(SLABS_PER_PIECE):
-                x_slabs.append(whole[:, :, h * SLAB_COLS : (h + 1) * SLAB_COLS])
+            x_images[image].append(whole)
+            x_cols[image] = LOAD_COLS
             if piece == 0:
                 nc.sync.dma_start(out=w_raw[:], in_=w_view)
         for image in range(IMAGES - WHOLE_IMAGES, IMAGES):
             x_image = image_pool.tile([P, PACK * PIXELS], BF16, name="x_image")
             whole = x_image[:].rearrange("p (t c) -> p t c", t=PACK)
             nc.sync.dma_start(out=whole, in_=x_view[image, :, :, :])
-            for h in range(PIXELS // SLAB_COLS):
-                x_slabs.append(whole[:, :, h * SLAB_COLS : (h + 1) * SLAB_COLS])
+            x_images[image].append(whole)
+            x_cols[image] = PIXELS
 
         pick_index = const.tile([P, LAYERS, COUT], I32)
         nc.gpsimd.iota(
@@ -128,31 +128,46 @@ def tile_conv_1x1_9_layer_kernel(tc, x, weights, biases, out):
                 in_=w_grouped[:].rearrange("p o t -> p (o t)"),
             )
 
+        slabs = []
+        for image in range(IMAGES):
+            for first in range(0, PIXELS, SLAB_COLS):
+                if image == IMAGES - 1 and first == PIXELS - SLAB_COLS:
+                    slabs.append((image, first, SLAB_COLS // 2))
+                    slabs.append((image, first + SLAB_COLS // 2, SLAB_COLS // 2))
+                else:
+                    slabs.append((image, first, SLAB_COLS))
+        stores = [(image, 0, PIXELS) for image in range(IMAGES - 1)]
+        first = 0
+        for cols in LAST_IMAGE_STORES:
+            stores.append((IMAGES - 1, first, cols))
+            first += cols
+        store_by_end = {(image, first + cols): (first, cols) for image, first, cols in stores}
+
         grouped = {}
         codes = {}
         scales = {}
         y_images = {}
 
         def regroup(s):
-            src = x_slabs[s]
-            dst = slab_pool.tile([P, SLAB_COLS, PACK], BF16, name="grouped", align_bytes=64)
+            image, first, cols = slabs[s]
+            src = x_images[image][first // x_cols[image]]
+            lo = first % x_cols[image]
+            split = cols * VECTOR_COLS // SLAB_COLS
+            dst = slab_pool.tile([P, cols, PACK], BF16, name="grouped", align_bytes=64)
             nc.vector.tensor_copy(
-                out=dst[:, 0:VECTOR_COLS, :].rearrange("p (c i) t -> p c t i", i=RUN),
-                in_=src[:, :, 0:VECTOR_COLS].rearrange(
-                    "p t (c i) -> p c t i", i=RUN
-                ),
+                out=dst[:, 0:split, :].rearrange("p (c i) t -> p c t i", i=RUN),
+                in_=src[:, :, lo : lo + split].rearrange("p t (c i) -> p c t i", i=RUN),
             )
             nc.scalar.copy(
-                out=dst[:, VECTOR_COLS:SLAB_COLS, :].rearrange("p (c i) t -> p c t i", i=RUN),
-                in_=src[:, :, VECTOR_COLS:SLAB_COLS].rearrange(
-                    "p t (c i) -> p c t i", i=RUN
-                ),
+                out=dst[:, split:cols, :].rearrange("p (c i) t -> p c t i", i=RUN),
+                in_=src[:, :, lo + split : lo + cols].rearrange("p t (c i) -> p c t i", i=RUN),
             )
             grouped[s] = dst
 
         def quantise(s):
-            codes[s] = slab_pool.tile([P, SLAB_COLS], U32, name="codes", align_bytes=64)
-            scales[s] = slab_pool.tile([P, SLAB_COLS], U8, name="scales", align_bytes=64)
+            cols = slabs[s][2]
+            codes[s] = slab_pool.tile([P, cols], U32, name="codes", align_bytes=64)
+            scales[s] = slab_pool.tile([P, cols], U8, name="scales", align_bytes=64)
             nc.vector.quantize_mx(
                 out=codes[s][:].bitcast(FP8X4),
                 scales=scales[s][:],
@@ -160,55 +175,39 @@ def tile_conv_1x1_9_layer_kernel(tc, x, weights, biases, out):
             )
 
         def multiply_and_store(s):
-            piece, part = divmod(s, SLABS_PER_PIECE)
-            image, image_part = divmod(piece, PIECES_PER_IMAGE)
-            if part == 0 and image_part == 0:
+            image, first, cols = slabs[s]
+            if first == 0:
                 y_images[image] = big_pool.tile([P, PIXELS], F32, name="big")
-            y_piece = y_images[image][:, image_part * LOAD_COLS : (image_part + 1) * LOAD_COLS]
-            for bank in range(BANKS_PER_SLAB):
-                cols = slice(bank * BANK_COLS, (bank + 1) * BANK_COLS)
+            y_image = y_images[image]
+            for lo in range(0, cols, BANK_COLS):
                 acc = acc_psum.tile([P, BANK_COLS], F32, name="acc")
                 nc.tensor.matmul_mx(
                     out=acc[:],
                     lhsT=w_codes[:].bitcast(FP8X4),
                     lhsT_scale=w_scales[:],
-                    rhs=codes[s][:, cols].bitcast(FP8X4),
-                    rhs_scale=scales[s][:, cols],
+                    rhs=codes[s][:, lo : lo + BANK_COLS].bitcast(FP8X4),
+                    rhs_scale=scales[s][:, lo : lo + BANK_COLS],
                     start=True,
                     stop=True,
                 )
-                first = part * SLAB_COLS + bank * BANK_COLS
-                if s == SLABS - 1 and bank == BANKS_PER_SLAB - 1:
-                    nc.vector.tensor_scalar_add(
-                        out=y_piece[:, first : first + BANK_COLS], in0=acc[:], scalar1=bias[:, 0:1]
-                    )
+                y_bank = y_image[:, first + lo : first + lo + BANK_COLS]
+                if s == len(slabs) - 1:
+                    nc.vector.tensor_scalar_add(out=y_bank, in0=acc[:], scalar1=bias[:, 0:1])
                 else:
                     nc.scalar.activation(
-                        out=y_piece[:, first : first + BANK_COLS],
-                        in_=acc[:],
-                        func=identity_fn,
-                        bias=bias[:, 0:1],
-                        scale=1.0,
+                        out=y_bank, in_=acc[:], func=identity_fn, bias=bias[:, 0:1], scale=1.0
                     )
-            if piece == PIECES - 1:
-                lo = part * SLAB_COLS
+            if (image, first + cols) in store_by_end:
+                store_first, store_cols = store_by_end[(image, first + cols)]
                 nc.sync.dma_start(
-                    out=y_view[image, :, image_part * LOAD_COLS + lo : image_part * LOAD_COLS + lo + SLAB_COLS],
-                    in_=y_piece[:, lo : lo + SLAB_COLS],
+                    out=y_view[image, :, store_first : store_first + store_cols],
+                    in_=y_image[:, store_first : store_first + store_cols],
                 )
-            elif image == IMAGES - 1:
-                if part == SLABS_PER_PIECE - 1:
-                    nc.sync.dma_start(
-                        out=y_view[image, :, image_part * LOAD_COLS : (image_part + 1) * LOAD_COLS],
-                        in_=y_piece,
-                    )
-            elif part == SLABS_PER_PIECE - 1 and image_part == PIECES_PER_IMAGE - 1:
-                nc.sync.dma_start(out=y_view[image, :, :], in_=y_images[image][:])
 
-        for step in range(SLABS + 2):
-            if step < SLABS:
+        for step in range(len(slabs) + 2):
+            if step < len(slabs):
                 regroup(step)
-            if 1 <= step <= SLABS:
+            if 1 <= step <= len(slabs):
                 quantise(step - 1)
             if step == WEIGHTS_STEP:
                 finish_weights()

@@ -22,7 +22,7 @@ assert CIN == P * PACK and COUT == P
 LOAD_COLS = 2048
 SLAB_COLS = 1024
 BANK_COLS = 512
-RUN = 4
+RUN = 8
 
 WEIGHTS_STEP = 2
 WHOLE_IMAGES = 2

@@ -35,6 +35,8 @@ VECTOR_COLS = 688
 
 BIG_BUFS = 6
 
+DMA_ALIGN = 256
+
 FLOPS = 2 * IMAGES * PIXELS * CIN * COUT
 
 
@@ -56,7 +58,7 @@ def tile_conv_1x1_9_layer_kernel(tc, x, weights, biases, out):
 
         ctx.enter_context(tc.manual_schedule())
 
-        w_raw = const.tile([P, LAYERS, CIN], BF16)
+        w_raw = const.tile([P, LAYERS, CIN], BF16, align_bytes=DMA_ALIGN)
         bias_rows = const.tile([P, COUT], BF16)
         nc.vector.memset(bias_rows[:], 0.0)
         nc.scalar.dma_start(out=bias_rows[0:LAYERS, :], in_=biases)
@@ -65,7 +67,7 @@ def tile_conv_1x1_9_layer_kernel(tc, x, weights, biases, out):
         x_cols = {}
         for piece in range(PIECES - WHOLE_IMAGES * PIECES_PER_IMAGE):
             image, part = divmod(piece, PIECES_PER_IMAGE)
-            x_piece = big_pool.tile([P, PACK * LOAD_COLS], BF16, name="big")
+            x_piece = big_pool.tile([P, PACK * LOAD_COLS], BF16, name="big", align_bytes=DMA_ALIGN)
             first = part * LOAD_COLS
             whole = x_piece[:].rearrange("p (t c) -> p t c", t=PACK)
             nc.sync.dma_start(out=whole, in_=x_view[image, :, :, first : first + LOAD_COLS])
@@ -74,7 +76,7 @@ def tile_conv_1x1_9_layer_kernel(tc, x, weights, biases, out):
             if piece == 0:
                 nc.sync.dma_start(out=w_raw[:], in_=w_view)
         for image in range(IMAGES - WHOLE_IMAGES, IMAGES):
-            x_image = image_pool.tile([P, PACK * PIXELS], BF16, name="x_image")
+            x_image = image_pool.tile([P, PACK * PIXELS], BF16, name="x_image", align_bytes=DMA_ALIGN)
             whole = x_image[:].rearrange("p (t c) -> p t c", t=PACK)
             nc.sync.dma_start(out=whole, in_=x_view[image, :, :, :])
             x_images[image].append(whole)
@@ -177,7 +179,7 @@ def tile_conv_1x1_9_layer_kernel(tc, x, weights, biases, out):
         def multiply_and_store(s):
             image, first, cols = slabs[s]
             if first == 0:
-                y_images[image] = big_pool.tile([P, PIXELS], F32, name="big")
+                y_images[image] = big_pool.tile([P, PIXELS], F32, name="big", align_bytes=DMA_ALIGN)
             y_image = y_images[image]
             for lo in range(0, cols, BANK_COLS):
                 acc = acc_psum.tile([P, BANK_COLS], F32, name="acc")

from contextlib import ExitStack

import concourse.mybir as mybir

BF16 = mybir.dt.bfloat16
F32 = mybir.dt.float32
I32 = mybir.dt.int32
U32 = mybir.dt.uint32
U8 = mybir.dt.uint8
FP8X4 = mybir.dt.float8_e4m3fn_x4

IMAGES = 4
CIN = 512
PIXELS = 64 * 64
COUT = 128
LAYERS = 9

P = 128
PACK = 4
assert CIN == P * PACK and COUT == P

LOAD_COLS = 2048
SLAB_COLS = 1024
BANK_COLS = 512
RUN = 8

WEIGHTS_STEP = 2
WHOLE_IMAGES = 2
PIECES = IMAGES * PIXELS // LOAD_COLS
PIECES_PER_IMAGE = PIXELS // LOAD_COLS
LAST_IMAGE_STORES = (2048, 1024, 512, 512)
assert sum(LAST_IMAGE_STORES) == PIXELS

VECTOR_COLS = 688

BIG_BUFS = 6

DMA_ALIGN = 256

FLOPS = 2 * IMAGES * PIXELS * CIN * COUT


def tile_conv_1x1_9_layer_kernel(tc, x, weights, biases, out):
    nc = tc.nc
    identity_fn = mybir.ActivationFunctionType.Identity

    x_view = x.rearrange("n (p t) h v -> n p t (h v)", t=PACK)
    w_view = weights.rearrange("i o c a b -> (i o) (c a b)").rearrange("(q j) c -> q j c", j=LAYERS)
    y_view = out.rearrange("n o h v -> n o (h v)")

    with ExitStack() as ctx:
        const = ctx.enter_context(tc.tile_pool(name="const", bufs=1))
        big_pool = ctx.enter_context(tc.tile_pool(name="big", bufs=BIG_BUFS))
        image_pool = ctx.enter_context(tc.tile_pool(name="image", bufs=WHOLE_IMAGES))
        slab_pool = ctx.enter_context(tc.tile_pool(name="slab", bufs=3))
        prep_psum = ctx.enter_context(tc.psum_pool(name="prep_psum", bufs=1))
        acc_psum = ctx.enter_context(tc.psum_pool(name="acc_psum", bufs=6))

        ctx.enter_context(tc.manual_schedule())

        w_raw = const.tile([P, LAYERS, CIN], BF16, align_bytes=DMA_ALIGN)
        bias_rows = const.tile([P, COUT], BF16)
        nc.vector.memset(bias_rows[:], 0.0)
        nc.scalar.dma_start(out=bias_rows[0:LAYERS, :], in_=biases)

        x_images = {image: [] for image in range(IMAGES)}
        x_cols = {}
        for piece in range(PIECES - WHOLE_IMAGES * PIECES_PER_IMAGE):
            image, part = divmod(piece, PIECES_PER_IMAGE)
            x_piece = big_pool.tile([P, PACK * LOAD_COLS], BF16, name="big", align_bytes=DMA_ALIGN)
            first = part * LOAD_COLS
            whole = x_piece[:].rearrange("p (t c) -> p t c", t=PACK)
            nc.sync.dma_start(out=whole, in_=x_view[image, :, :, first : first + LOAD_COLS])
            x_images[image].append(whole)
            x_cols[image] = LOAD_COLS
            if piece == 0:
                nc.sync.dma_start(out=w_raw[:], in_=w_view)
        for image in range(IMAGES - WHOLE_IMAGES, IMAGES):
            x_image = image_pool.tile([P, PACK * PIXELS], BF16, name="x_image", align_bytes=DMA_ALIGN)
            whole = x_image[:].rearrange("p (t c) -> p t c", t=PACK)
            nc.sync.dma_start(out=whole, in_=x_view[image, :, :, :])
            x_images[image].append(whole)
            x_cols[image] = PIXELS

        pick_index = const.tile([P, LAYERS, COUT], I32)
        nc.gpsimd.iota(
            pick_index[:], pattern=[[1, LAYERS], [-1, COUT]], base=COUT, channel_multiplier=LAYERS
        )
        pick_low = const.tile([P, LAYERS, COUT], I32)
        nc.vector.tensor_scalar(
            out=pick_low[:],
            in0=pick_index[:],
            scalar1=COUT - 1,
            scalar2=None,
            op0=mybir.AluOpType.bitwise_and,
        )
        pick = const.tile([P, LAYERS, COUT], BF16)
        nc.vector.tensor_scalar(
            out=pick[:], in0=pick_low[:], scalar1=0.0, scalar2=None, op0=mybir.AluOpType.is_equal
        )
        w_by_code = w_raw[:].rearrange("q j (p t) -> q j t p", t=PACK)
        w_sum = prep_psum.tile([P, PACK, COUT], F32)
        for t in range(PACK):
            for j in range(LAYERS):
                nc.tensor.matmul(
                    out=w_sum[:, t, :],
                    lhsT=w_by_code[:, j, t, :],
                    rhs=pick[:, j, :],
                    start=(j == 0),
                    stop=(j == LAYERS - 1),
                )
        ones = const.tile([P, P], BF16)
        nc.vector.memset(ones[:], 1.0)
        bias_sum = prep_psum.tile([P, P], F32)
        nc.tensor.matmul(out=bias_sum[:], lhsT=bias_rows[:], rhs=ones[:], start=True, stop=True)

        w_grouped = const.tile([P, COUT, PACK], BF16, align_bytes=64)
        w_codes = const.tile([P, COUT], U32, align_bytes=64)
        w_scales = const.tile([P, COUT], U8, align_bytes=64)
        bias = const.tile([P, 1], F32)

        def finish_weights():
            nc.vector.tensor_scalar_mul(
                out=w_grouped[:], in0=w_sum[:].rearrange("p t o -> p o t"), scalar1=1.0 / LAYERS
            )
            nc.vector.tensor_scalar_mul(out=bias[:], in0=bias_sum[:, 0:1], scalar1=1.0 / LAYERS)
            nc.vector.quantize_mx(
                out=w_codes[:].bitcast(FP8X4),
                scales=w_scales[:],
                in_=w_grouped[:].rearrange("p o t -> p (o t)"),
            )

        slabs = []
        for image in range(IMAGES):
            for first in range(0, PIXELS, SLAB_COLS):
                if image == IMAGES - 1 and first == PIXELS - SLAB_COLS:
                    slabs.append((image, first, SLAB_COLS // 2))
                    slabs.append((image, first + SLAB_COLS // 2, SLAB_COLS // 2))
                else:
                    slabs.append((image, first, SLAB_COLS))
        stores = [(image, 0, PIXELS) for image in range(IMAGES - 1)]
        first = 0
        for cols in LAST_IMAGE_STORES:
            stores.append((IMAGES - 1, first, cols))
            first += cols
        store_by_end = {(image, first + cols): (first, cols) for image, first, cols in stores}

        grouped = {}
        codes = {}
        scales = {}
        y_images = {}

        def regroup(s):
            image, first, cols = slabs[s]
            src = x_images[image][first // x_cols[image]]
            lo = first % x_cols[image]
            split = cols * VECTOR_COLS // SLAB_COLS
            dst = slab_pool.tile([P, cols, PACK], BF16, name="grouped", align_bytes=64)
            nc.vector.tensor_copy(
                out=dst[:, 0:split, :].rearrange("p (c i) t -> p c t i", i=RUN),
                in_=src[:, :, lo : lo + split].rearrange("p t (c i) -> p c t i", i=RUN),
            )
            nc.scalar.copy(
                out=dst[:, split:cols, :].rearrange("p (c i) t -> p c t i", i=RUN),
                in_=src[:, :, lo + split : lo + cols].rearrange("p t (c i) -> p c t i", i=RUN),
            )
            grouped[s] = dst

        def quantise(s):
            cols = slabs[s][2]
            codes[s] = slab_pool.tile([P, cols], U32, name="codes", align_bytes=64)
            scales[s] = slab_pool.tile([P, cols], U8, name="scales", align_bytes=64)
            nc.vector.quantize_mx(
                out=codes[s][:].bitcast(FP8X4),
                scales=scales[s][:],
                in_=grouped[s][:].rearrange("p c t -> p (c t)"),
            )

        def multiply_and_store(s):
            image, first, cols = slabs[s]
            if first == 0:
                y_images[image] = big_pool.tile([P, PIXELS], F32, name="big", align_bytes=DMA_ALIGN)
            y_image = y_images[image]
            for lo in range(0, cols, BANK_COLS):
                acc = acc_psum.tile([P, BANK_COLS], F32, name="acc")
                nc.tensor.matmul_mx(
                    out=acc[:],
                    lhsT=w_codes[:].bitcast(FP8X4),
                    lhsT_scale=w_scales[:],
                    rhs=codes[s][:, lo : lo + BANK_COLS].bitcast(FP8X4),
                    rhs_scale=scales[s][:, lo : lo + BANK_COLS],
                    start=True,
                    stop=True,
                )
                y_bank = y_image[:, first + lo : first + lo + BANK_COLS]
                if s == len(slabs) - 1:
                    nc.vector.tensor_scalar_add(out=y_bank, in0=acc[:], scalar1=bias[:, 0:1])
                else:
                    nc.scalar.activation(
                        out=y_bank, in_=acc[:], func=identity_fn, bias=bias[:, 0:1], scale=1.0
                    )
            if (image, first + cols) in store_by_end:
                store_first, store_cols = store_by_end[(image, first + cols)]
                nc.sync.dma_start(
                    out=y_view[image, :, store_first : store_first + store_cols],
                    in_=y_image[:, store_first : store_first + store_cols],
                )

        for step in range(len(slabs) + 2):
            if step < len(slabs):
                regroup(step)
            if 1 <= step <= len(slabs):
                quantise(step - 1)
            if step == WEIGHTS_STEP:
                finish_weights()
            if step == WEIGHTS_STEP + 1:
                multiply_and_store(step - 3)
            if step > WEIGHTS_STEP:
                multiply_and_store(step - 2)
